import numpy as np
import ml_dtypes


def mxq(x, axis, fmt="e4m3"):
    dtype, down = {"e4m3": (ml_dtypes.float8_e4m3fn, 7), "e5m2": (ml_dtypes.float8_e5m2, 14)}[fmt]
    v = np.moveaxis(np.asarray(x, np.float32).astype(ml_dtypes.bfloat16).astype(np.float64), axis, -1)
    blocks = v.reshape(v.shape[:-1] + (-1, 32))
    amax = np.abs(blocks).max(-1, keepdims=True)
    byte = np.maximum(np.where(amax > 0, np.frexp(amax)[1] - 1 + 127, 0) - down, 1)
    scale = np.exp2(byte - 127.0)
    codes = (blocks / scale).astype(np.float32).astype(dtype).astype(np.float64)
    return np.moveaxis((codes * scale).reshape(v.shape), -1, axis)


WIDE = False


def mx_kscale(k):
    if not WIDE:
        return np.ones(k)
    levels = np.array([10, -10, 5, -5, 0])
    a = np.random.permutation(np.resize(levels, k // 512 * 4)).reshape(k // 512, 4)
    idx = np.arange(k)
    return np.exp2(a[idx // 512, idx % 128 // 32])


BF16 = ml_dtypes.bfloat16


def bf(x):
    return np.asarray(x, np.float32).astype(BF16)


def f64(x):
    return np.asarray(x).astype(np.float64)


B, S, IN_DIM, UNITS = 2, 256, 16384, 512
EPS = 1e-6


def _ternary_kernel():
    limit = np.sqrt(6.0 / (IN_DIM + UNITS))
    w = np.random.uniform(-limit, limit, (IN_DIM, UNITS))
    scale = np.mean(np.abs(w)) + EPS
    return np.clip(np.round(w / scale), -1.0, 1.0)


def setup_inputs():
    s = mx_kscale(IN_DIM)
    return {"x": bf(np.random.standard_normal((B, S, IN_DIM)) * (1.2 / np.sqrt(IN_DIM)) * s),
            "kernel": bf(_ternary_kernel() / s[:, None]),
            "bias": bf(np.random.standard_normal(UNITS) * 0.1)}


def reference(x, kernel, bias):
    return (mxq(f64(x), 2, "e4m3") @ mxq(f64(kernel), 0, "e4m3")) + f64(bias)

@@ -1,0 +1,206 @@
+from contextlib import ExitStack
+
+import concourse.mybir as mybir
+from concourse.masks import make_identity
+
+F32 = mybir.dt.float32
+BF16 = mybir.dt.bfloat16
+U32 = mybir.dt.uint32
+U8 = mybir.dt.uint8
+FP8X4 = mybir.dt.float8_e4m3fn_x4
+
+P = 128
+PACK = 4
+K_PASS = P * PACK
+ROWS = 512
+K = 16384
+N = 512
+M_TILES = ROWS // P
+PASSES = K // K_PASS
+CHUNK_PASSES = 4
+CHUNK_K = CHUNK_PASSES * K_PASS
+BANK_PASSES = 2
+
+PER_ROUND = 1
+ROUNDS = PASSES // PER_ROUND
+LEAD = CHUNK_PASSES // PER_ROUND
+RAW_BUFS = 8
+SCALAR_COLS = 192
+
+FLOPS = 2 * ROWS * K * N
+
+
+def tile_bitlinear_k_kernel(tc, x, kernel, bias, out):
+    nc = tc.nc
+    x_rows = x.flatten_outer_dims()
+    out_rows = out.flatten_outer_dims()
+
+    with ExitStack() as ctx:
+        const = ctx.enter_context(tc.tile_pool(name="const", bufs=1))
+        raw = ctx.enter_context(tc.tile_pool(name="raw", bufs=RAW_BUFS))
+        grouped = ctx.enter_context(tc.tile_pool(name="grouped", bufs=3))
+        x_quant = ctx.enter_context(tc.tile_pool(name="x_quant", bufs=2 * LEAD))
+        w_quant = ctx.enter_context(tc.tile_pool(name="w_quant", bufs=3))
+        results = ctx.enter_context(tc.tile_pool(name="results", bufs=M_TILES))
+        psum_t = ctx.enter_context(tc.psum_pool(name="psum_t", bufs=4))
+        psum_acc = ctx.enter_context(tc.psum_pool(name="psum_acc", bufs=1))
+        ctx.enter_context(tc.manual_schedule())
+
+        x_raw_of = {}
+        w_raw_of = {}
+        banks_of = {}
+        x_grouped_of = {}
+        w_grouped_of = {}
+        x_codes_of = {}
+        x_scales_of = {}
+        w_codes_of = {}
+        w_scales_of = {}
+
+        def load_x(xi):
+            x_raw = raw.tile([P, PER_ROUND, CHUNK_K], BF16)
+            for i in range(PER_ROUND):
+                chunk, m = divmod(xi * PER_ROUND + i, M_TILES)
+                nc.sync.dma_start(
+                    out=x_raw[:, i, :],
+                    in_=x_rows[m * P : (m + 1) * P, chunk * CHUNK_K : (chunk + 1) * CHUNK_K],
+                )
+            x_raw_of[xi] = x_raw
+
+        def load_w(n):
+            w_raw = raw.tile([P, PER_ROUND, PACK, N], BF16)
+            for i in range(PER_ROUND):
+                g = n * PER_ROUND + i
+                nc.sync.dma_start(
+                    out=w_raw[:, i].rearrange("p (u e) n -> p u e n", e=2),
+                    in_=kernel[g * K_PASS : (g + 1) * K_PASS, :].rearrange(
+                        "(u q e) n -> q u e n", u=2, e=2
+                    ),
+                )
+            w_raw_of[n] = w_raw
+
+        def load_group(n):
+            if n + LEAD < ROUNDS:
+                load_x(n + LEAD)
+            if 0 <= n < ROUNDS:
+                load_w(n)
+
+        def transpose_x(xi):
+            banks = []
+            for i in range(PER_ROUND):
+                words = x_raw_of[xi][:, i, :].bitcast(F32)
+                for b in range(CHUNK_PASSES // BANK_PASSES):
+                    bank = psum_t.tile([P, BANK_PASSES, 2, P], F32, tag="bank")
+                    for a in range(BANK_PASSES):
+                        for u in range(2):
+                            j = (b * BANK_PASSES + a) * 2 + u
+                            nc.tensor.transpose(
+                                bank[:, a, u, :], words[:, j * P : (j + 1) * P], ident[:]
+                            )
+                    banks.append(bank)
+            banks_of[xi] = banks
+
+        def copy_x(xi):
+            x_grouped = grouped.tile([P, PER_ROUND, CHUNK_PASSES, P, PACK], BF16, align_bytes=64)
+            for i in range(PER_ROUND):
+                for b in range(CHUNK_PASSES // BANK_PASSES):
+                    bank = banks_of[xi][i * (CHUNK_PASSES // BANK_PASSES) + b]
+                    nc.scalar.copy(
+                        out=x_grouped[:, i, b * BANK_PASSES : (b + 1) * BANK_PASSES].bitcast(F32),
+                        in_=bank[:].rearrange("p a u r -> p a r u"),
+                    )
+            x_grouped_of[xi] = x_grouped
+
+        def quantise_x(xi):
+            x_codes = x_quant.tile([P, PER_ROUND, CHUNK_PASSES, P], U32, align_bytes=64)
+            x_scales = x_quant.tile([P, PER_ROUND, CHUNK_PASSES, P], U8, align_bytes=64)
+            nc.vector.quantize_mx(
+                out=x_codes[:].rearrange("p i a r -> p (i a r)").bitcast(FP8X4),
+                scales=x_scales[:].rearrange("p i a r -> p (i a r)"),
+                in_=x_grouped_of[xi][:].rearrange("p i a r t -> p (i a r t)"),
+            )
+            x_codes_of[xi] = x_codes
+            x_scales_of[xi] = x_scales
+
+        def regroup_w(n):
+            w_grouped = grouped.tile([P, PER_ROUND, N, PACK], BF16, align_bytes=64)
+            w_raw = w_raw_of[n]
+            for i in range(PER_ROUND):
+                nc.scalar.copy(
+                    out=w_grouped[:, i, :SCALAR_COLS, :].rearrange("p (c j) t -> p c t j", j=4),
+                    in_=w_raw[:, i, :, :SCALAR_COLS].rearrange("p t (c j) -> p c t j", j=4),
+                )
+                nc.vector.tensor_copy(
+                    out=w_grouped[:, i, SCALAR_COLS:, :].rearrange("p (c j) t -> p c t j", j=4),
+                    in_=w_raw[:, i, :, SCALAR_COLS:].rearrange("p t (c j) -> p c t j", j=4),
+                )
+            w_grouped_of[n] = w_grouped
+
+        def quantise_w(n):
+            w_codes = w_quant.tile([P, PER_ROUND, N], U32, align_bytes=64)
+            w_scales = w_quant.tile([P, PER_ROUND, N], U8, align_bytes=64)
+            nc.vector.quantize_mx(
+                out=w_codes[:].rearrange("p i n -> p (i n)").bitcast(FP8X4),
+                scales=w_scales[:].rearrange("p i n -> p (i n)"),
+                in_=w_grouped_of[n][:].rearrange("p i n t -> p (i n t)"),
+            )
+            w_codes_of[n] = w_codes
+            w_scales_of[n] = w_scales
+
+        def multiply(n):
+            for i in range(PER_ROUND):
+                g = n * PER_ROUND + i
+                chunk, a = divmod(g, CHUNK_PASSES)
+                for m in range(M_TILES):
+                    xi, xs = divmod(chunk * M_TILES + m, PER_ROUND)
+                    nc.tensor.matmul_mx(
+                        out=acc[m][:],
+                        lhsT=x_codes_of[xi][:, xs, a, :].bitcast(FP8X4),
+                        lhsT_scale=x_scales_of[xi][:, xs, a, :],
+                        rhs=w_codes_of[n][:, i, :].bitcast(FP8X4),
+                        rhs_scale=w_scales_of[n][:, i, :],
+                        start=(g == 0),
+                        stop=(g == PASSES - 1),
+                    )
+
+        for n in range(-LEAD, RAW_BUFS - LEAD):
+            load_group(n)
+
+        ident = const.tile([P, P], F32)
+        make_identity(nc, ident[:])
+
+        ones = const.tile([P, P], BF16)
+        nc.vector.memset(ones[:], 1.0)
+        bias_row = const.tile([P, N], BF16)
+        nc.vector.memset(bias_row[:], 0.0)
+        nc.scalar.dma_start(out=bias_row[0:1, :], in_=bias.rearrange("(o n) -> o n", o=1))
+        bias_bank = psum_t.tile([P, N], F32, tag="bank")
+        nc.tensor.matmul(out=bias_bank[:], lhsT=ones[:], rhs=bias_row[:], start=True, stop=True)
+        bias_all = const.tile([P, N], F32)
+        nc.vector.tensor_copy(out=bias_all[:], in_=bias_bank[:])
+
+        acc = []
+        for m in range(M_TILES):
+            acc_m = psum_acc.tile([P, N], F32, name="acc%d" % m)
+            acc.append(acc_m)
+
+        for n in range(-LEAD, ROUNDS):
+            xi = n + LEAD
+            if xi < ROUNDS:
+                transpose_x(xi)
+            if n >= 0:
+                regroup_w(n)
+            if xi < ROUNDS:
+                copy_x(xi)
+            if 0 <= xi - 1 < ROUNDS:
+                quantise_x(xi - 1)
+            if n >= 0:
+                quantise_w(n)
+                multiply(n)
+            load_group(n + RAW_BUFS)
+
+        for m in range(M_TILES):
+            result = results.tile([P, N], F32)
+            nc.vector.tensor_tensor(
+                out=result[:], in0=acc[m][:], in1=bias_all[:], op=mybir.AluOpType.add
+            )
+            nc.sync.dma_start(out=out_rows[m * P : (m + 1) * P, :], in_=result[:])

@@ -79,8 +79,8 @@ def tile_bitlinear_k_kernel(tc, x, kernel, bias, out):
             w_raw_of[n] = w_raw
 
         def load_group(n):
-            if n + LEAD < ROUNDS:
-                load_x(n + LEAD)
+            if n + LEAD + 1 < ROUNDS:
+                load_x(n + LEAD + 1)
             if 0 <= n < ROUNDS:
                 load_w(n)
 
@@ -162,41 +162,46 @@ def tile_bitlinear_k_kernel(tc, x, kernel, bias, out):
                         stop=(g == PASSES - 1),
                     )
 
-        for n in range(-LEAD, RAW_BUFS - LEAD):
+        def step(n):
+            if n + LEAD + 1 < ROUNDS:
+                transpose_x(n + LEAD + 1)
+            if n >= 0:
+                regroup_w(n)
+            if 0 <= n + LEAD < ROUNDS:
+                copy_x(n + LEAD)
+            if 0 <= n + LEAD - 1 < ROUNDS:
+                quantise_x(n + LEAD - 1)
+            if n >= 0:
+                quantise_w(n)
+                multiply(n)
+            load_group(n + RAW_BUFS)
+
+        first_step = -(LEAD + 1)
+        for n in range(first_step, first_step + RAW_BUFS):
             load_group(n)
 
         ident = const.tile([P, P], F32)
         make_identity(nc, ident[:])
-
         ones = const.tile([P, P], BF16)
         nc.vector.memset(ones[:], 1.0)
         bias_row = const.tile([P, N], BF16)
         nc.vector.memset(bias_row[:], 0.0)
         nc.scalar.dma_start(out=bias_row[0:1, :], in_=bias.rearrange("(o n) -> o n", o=1))
-        bias_bank = psum_t.tile([P, N], F32, tag="bank")
-        nc.tensor.matmul(out=bias_bank[:], lhsT=ones[:], rhs=bias_row[:], start=True, stop=True)
-        bias_all = const.tile([P, N], F32)
-        nc.vector.tensor_copy(out=bias_all[:], in_=bias_bank[:])
 
         acc = []
         for m in range(M_TILES):
             acc_m = psum_acc.tile([P, N], F32, name="acc%d" % m)
             acc.append(acc_m)
 
-        for n in range(-LEAD, ROUNDS):
-            xi = n + LEAD
-            if xi < ROUNDS:
-                transpose_x(xi)
-            if n >= 0:
-                regroup_w(n)
-            if xi < ROUNDS:
-                copy_x(xi)
-            if 0 <= xi - 1 < ROUNDS:
-                quantise_x(xi - 1)
-            if n >= 0:
-                quantise_w(n)
-                multiply(n)
-            load_group(n + RAW_BUFS)
+        for n in range(first_step, 0):
+            step(n)
+
+        nc.tensor.matmul(out=acc[0][:], lhsT=ones[:], rhs=bias_row[:], start=True, stop=True)
+        bias_all = const.tile([P, N], F32)
+        nc.vector.tensor_copy(out=bias_all[:], in_=acc[0][:])
+
+        for n in range(ROUNDS):
+            step(n)
 
         for m in range(M_TILES):
             result = results.tile([P, N], F32)

@@ -25,7 +25,7 @@ PER_ROUND = 1
 ROUNDS = PASSES // PER_ROUND
 LEAD = CHUNK_PASSES // PER_ROUND
 RAW_BUFS = 8
-SCALAR_COLS = 192
+SCALAR_COLS = 128
 
 FLOPS = 2 * ROWS * K * N
 

@@ -11,6 +11,7 @@ FP8X4 = mybir.dt.float8_e4m3fn_x4
 
 P = 128
 PACK = 4
+HALVES = 2
 K_PASS = P * PACK
 ROWS = 512
 K = 16384
@@ -19,13 +20,17 @@ M_TILES = ROWS // P
 PASSES = K // K_PASS
 CHUNK_PASSES = 4
 CHUNK_K = CHUNK_PASSES * K_PASS
+UNITS = M_TILES * (PASSES // CHUNK_PASSES)
 BANK_PASSES = 2
+UNIT_BANKS = CHUNK_PASSES // BANK_PASSES
 
-PER_ROUND = 1
-ROUNDS = PASSES // PER_ROUND
-LEAD = CHUNK_PASSES // PER_ROUND
-RAW_BUFS = 8
-SCALAR_COLS = 128
+QUANTISE_AHEAD = M_TILES - 1
+COPY_AHEAD = QUANTISE_AHEAD + 1
+TRANSPOSE_AHEAD = COPY_AHEAD + 1
+X_BUFS = 8
+GROUPS_AHEAD = X_BUFS + TRANSPOSE_AHEAD - QUANTISE_AHEAD
+W_BUFS = GROUPS_AHEAD
+SCALAR_COLS = 192
 
 FLOPS = 2 * ROWS * K * N
 
@@ -37,12 +42,13 @@ def tile_bitlinear_k_kernel(tc, x, kernel, bias, out):
 
     with ExitStack() as ctx:
         const = ctx.enter_context(tc.tile_pool(name="const", bufs=1))
-        raw = ctx.enter_context(tc.tile_pool(name="raw", bufs=RAW_BUFS))
+        x_loaded = ctx.enter_context(tc.tile_pool(name="x_loaded", bufs=X_BUFS))
+        w_loaded = ctx.enter_context(tc.tile_pool(name="w_loaded", bufs=W_BUFS))
         grouped = ctx.enter_context(tc.tile_pool(name="grouped", bufs=3))
-        x_quant = ctx.enter_context(tc.tile_pool(name="x_quant", bufs=2 * LEAD))
         w_quant = ctx.enter_context(tc.tile_pool(name="w_quant", bufs=3))
+        x_quant = ctx.enter_context(tc.tile_pool(name="x_quant", bufs=2 * M_TILES))
         results = ctx.enter_context(tc.tile_pool(name="results", bufs=M_TILES))
-        psum_t = ctx.enter_context(tc.psum_pool(name="psum_t", bufs=4))
+        psum_t = ctx.enter_context(tc.psum_pool(name="psum_t", bufs=2 * UNIT_BANKS))
         psum_acc = ctx.enter_context(tc.psum_pool(name="psum_acc", bufs=1))
         ctx.enter_context(tc.manual_schedule())
 
@@ -56,129 +62,120 @@ def tile_bitlinear_k_kernel(tc, x, kernel, bias, out):
         w_codes_of = {}
         w_scales_of = {}
 
-        def load_x(xi):
-            x_raw = raw.tile([P, PER_ROUND, CHUNK_K], BF16)
-            for i in range(PER_ROUND):
-                chunk, m = divmod(xi * PER_ROUND + i, M_TILES)
-                nc.sync.dma_start(
-                    out=x_raw[:, i, :],
-                    in_=x_rows[m * P : (m + 1) * P, chunk * CHUNK_K : (chunk + 1) * CHUNK_K],
-                )
-            x_raw_of[xi] = x_raw
+        def load_x(unit):
+            chunk, m = divmod(unit, M_TILES)
+            x_raw = x_loaded.tile([P, CHUNK_K], BF16)
+            nc.sync.dma_start(
+                out=x_raw[:],
+                in_=x_rows[m * P : (m + 1) * P, chunk * CHUNK_K : (chunk + 1) * CHUNK_K],
+            )
+            x_raw_of[unit] = x_raw
 
-        def load_w(n):
-            w_raw = raw.tile([P, PER_ROUND, PACK, N], BF16)
-            for i in range(PER_ROUND):
-                g = n * PER_ROUND + i
-                nc.sync.dma_start(
-                    out=w_raw[:, i].rearrange("p (u e) n -> p u e n", e=2),
-                    in_=kernel[g * K_PASS : (g + 1) * K_PASS, :].rearrange(
-                        "(u q e) n -> q u e n", u=2, e=2
-                    ),
-                )
-            w_raw_of[n] = w_raw
+        def load_w(g):
+            w_raw = w_loaded.tile([P, PACK, N], BF16)
+            nc.sync.dma_start(
+                out=w_raw[:].rearrange("p (h e) n -> p h e n", h=HALVES),
+                in_=kernel[g * K_PASS : (g + 1) * K_PASS, :].rearrange(
+                    "(h p e) n -> p h e n", h=HALVES, p=P
+                ),
+            )
+            w_raw_of[g] = w_raw
 
-        def load_group(n):
-            if n + LEAD + 1 < ROUNDS:
-                load_x(n + LEAD + 1)
-            if 0 <= n < ROUNDS:
-                load_w(n)
+        def load_group(g):
+            if 0 <= g + QUANTISE_AHEAD < UNITS:
+                load_x(g + QUANTISE_AHEAD)
+            if 0 <= g < PASSES:
+                load_w(g)
 
-        def transpose_x(xi):
+        def transpose_x(unit):
+            words = x_raw_of[unit][:].bitcast(F32)
             banks = []
-            for i in range(PER_ROUND):
-                words = x_raw_of[xi][:, i, :].bitcast(F32)
-                for b in range(CHUNK_PASSES // BANK_PASSES):
-                    bank = psum_t.tile([P, BANK_PASSES, 2, P], F32, tag="bank")
-                    for a in range(BANK_PASSES):
-                        for u in range(2):
-                            j = (b * BANK_PASSES + a) * 2 + u
-                            nc.tensor.transpose(
-                                bank[:, a, u, :], words[:, j * P : (j + 1) * P], ident[:]
-                            )
-                    banks.append(bank)
-            banks_of[xi] = banks
+            for b in range(UNIT_BANKS):
+                bank = psum_t.tile([P, BANK_PASSES, HALVES, P], F32)
+                for a in range(BANK_PASSES):
+                    for h in range(HALVES):
+                        j = (b * BANK_PASSES + a) * HALVES + h
+                        nc.tensor.transpose(
+                            bank[:, a, h, :], words[:, j * P : (j + 1) * P], ident[:]
+                        )
+                banks.append(bank)
+            banks_of[unit] = banks
 
-        def copy_x(xi):
-            x_grouped = grouped.tile([P, PER_ROUND, CHUNK_PASSES, P, PACK], BF16, align_bytes=64)
-            for i in range(PER_ROUND):
-                for b in range(CHUNK_PASSES // BANK_PASSES):
-                    bank = banks_of[xi][i * (CHUNK_PASSES // BANK_PASSES) + b]
-                    nc.scalar.copy(
-                        out=x_grouped[:, i, b * BANK_PASSES : (b + 1) * BANK_PASSES].bitcast(F32),
-                        in_=bank[:].rearrange("p a u r -> p a r u"),
-                    )
-            x_grouped_of[xi] = x_grouped
-
-        def quantise_x(xi):
-            x_codes = x_quant.tile([P, PER_ROUND, CHUNK_PASSES, P], U32, align_bytes=64)
-            x_scales = x_quant.tile([P, PER_ROUND, CHUNK_PASSES, P], U8, align_bytes=64)
-            nc.vector.quantize_mx(
-                out=x_codes[:].rearrange("p i a r -> p (i a r)").bitcast(FP8X4),
-                scales=x_scales[:].rearrange("p i a r -> p (i a r)"),
-                in_=x_grouped_of[xi][:].rearrange("p i a r t -> p (i a r t)"),
-            )
-            x_codes_of[xi] = x_codes
-            x_scales_of[xi] = x_scales
-
-        def regroup_w(n):
-            w_grouped = grouped.tile([P, PER_ROUND, N, PACK], BF16, align_bytes=64)
-            w_raw = w_raw_of[n]
-            for i in range(PER_ROUND):
+        def copy_x(unit):
+            x_grouped = grouped.tile([P, CHUNK_PASSES, P, PACK], BF16, align_bytes=64)
+            for b in range(UNIT_BANKS):
                 nc.scalar.copy(
-                    out=w_grouped[:, i, :SCALAR_COLS, :].rearrange("p (c j) t -> p c t j", j=4),
-                    in_=w_raw[:, i, :, :SCALAR_COLS].rearrange("p t (c j) -> p c t j", j=4),
+                    out=x_grouped[:, b * BANK_PASSES : (b + 1) * BANK_PASSES].bitcast(F32),
+                    in_=banks_of[unit][b][:].rearrange("p a h r -> p a r h"),
                 )
-                nc.vector.tensor_copy(
-                    out=w_grouped[:, i, SCALAR_COLS:, :].rearrange("p (c j) t -> p c t j", j=4),
-                    in_=w_raw[:, i, :, SCALAR_COLS:].rearrange("p t (c j) -> p c t j", j=4),
-                )
-            w_grouped_of[n] = w_grouped
+            x_grouped_of[unit] = x_grouped
 
-        def quantise_w(n):
-            w_codes = w_quant.tile([P, PER_ROUND, N], U32, align_bytes=64)
-            w_scales = w_quant.tile([P, PER_ROUND, N], U8, align_bytes=64)
+        def quantise_x(unit):
+            x_codes = x_quant.tile([P, CHUNK_PASSES, P], U32, align_bytes=64)
+            x_scales = x_quant.tile([P, CHUNK_PASSES, P], U8, align_bytes=64)
             nc.vector.quantize_mx(
-                out=w_codes[:].rearrange("p i n -> p (i n)").bitcast(FP8X4),
-                scales=w_scales[:].rearrange("p i n -> p (i n)"),
-                in_=w_grouped_of[n][:].rearrange("p i n t -> p (i n t)"),
+                out=x_codes[:].rearrange("p a r -> p (a r)").bitcast(FP8X4),
+                scales=x_scales[:].rearrange("p a r -> p (a r)"),
+                in_=x_grouped_of[unit][:].rearrange("p a r t -> p (a r t)"),
             )
-            w_codes_of[n] = w_codes
-            w_scales_of[n] = w_scales
+            x_codes_of[unit] = x_codes
+            x_scales_of[unit] = x_scales
 
-        def multiply(n):
-            for i in range(PER_ROUND):
-                g = n * PER_ROUND + i
-                chunk, a = divmod(g, CHUNK_PASSES)
-                for m in range(M_TILES):
-                    xi, xs = divmod(chunk * M_TILES + m, PER_ROUND)
-                    nc.tensor.matmul_mx(
-                        out=acc[m][:],
-                        lhsT=x_codes_of[xi][:, xs, a, :].bitcast(FP8X4),
-                        lhsT_scale=x_scales_of[xi][:, xs, a, :],
-                        rhs=w_codes_of[n][:, i, :].bitcast(FP8X4),
-                        rhs_scale=w_scales_of[n][:, i, :],
-                        start=(g == 0),
-                        stop=(g == PASSES - 1),
-                    )
+        def regroup_w(g):
+            w_raw = w_raw_of[g]
+            w_grouped = grouped.tile([P, N, PACK], BF16, align_bytes=64)
+            nc.scalar.copy(
+                out=w_grouped[:, :SCALAR_COLS, :].rearrange("p (c j) t -> p c t j", j=4),
+                in_=w_raw[:, :, :SCALAR_COLS].rearrange("p t (c j) -> p c t j", j=4),
+            )
+            nc.vector.tensor_copy(
+                out=w_grouped[:, SCALAR_COLS:, :].rearrange("p (c j) t -> p c t j", j=4),
+                in_=w_raw[:, :, SCALAR_COLS:].rearrange("p t (c j) -> p c t j", j=4),
+            )
+            w_grouped_of[g] = w_grouped
+
+        def quantise_w(g):
+            w_codes = w_quant.tile([P, N], U32, align_bytes=64)
+            w_scales = w_quant.tile([P, N], U8, align_bytes=64)
+            nc.vector.quantize_mx(
+                out=w_codes[:].bitcast(FP8X4),
+                scales=w_scales[:],
+                in_=w_grouped_of[g][:].rearrange("p n t -> p (n t)"),
+            )
+            w_codes_of[g] = w_codes
+            w_scales_of[g] = w_scales
+
+        def multiply(g):
+            chunk, a = divmod(g, CHUNK_PASSES)
+            for m in range(M_TILES):
+                unit = chunk * M_TILES + m
+                nc.tensor.matmul_mx(
+                    out=acc[m][:],
+                    lhsT=x_codes_of[unit][:, a, :].bitcast(FP8X4),
+                    lhsT_scale=x_scales_of[unit][:, a, :],
+                    rhs=w_codes_of[g][:].bitcast(FP8X4),
+                    rhs_scale=w_scales_of[g][:],
+                    start=(g == 0),
+                    stop=(g == PASSES - 1),
+                )
 
         def step(n):
-            if n + LEAD + 1 < ROUNDS:
-                transpose_x(n + LEAD + 1)
+            if n + TRANSPOSE_AHEAD < UNITS:
+                transpose_x(n + TRANSPOSE_AHEAD)
             if n >= 0:
                 regroup_w(n)
-            if 0 <= n + LEAD < ROUNDS:
-                copy_x(n + LEAD)
-            if 0 <= n + LEAD - 1 < ROUNDS:
-                quantise_x(n + LEAD - 1)
+            if 0 <= n + COPY_AHEAD < UNITS:
+                copy_x(n + COPY_AHEAD)
+            if 0 <= n + QUANTISE_AHEAD < UNITS:
+                quantise_x(n + QUANTISE_AHEAD)
             if n >= 0:
                 quantise_w(n)
                 multiply(n)
-            load_group(n + RAW_BUFS)
+            load_group(n + GROUPS_AHEAD)
 
-        first_step = -(LEAD + 1)
-        for n in range(first_step, first_step + RAW_BUFS):
-            load_group(n)
+        first_step = -TRANSPOSE_AHEAD
+        for g in range(first_step, first_step + GROUPS_AHEAD):
+            load_group(g)
 
         ident = const.tile([P, P], F32)
         make_identity(nc, ident[:])
@@ -200,7 +197,7 @@ def tile_bitlinear_k_kernel(tc, x, kernel, bias, out):
         bias_all = const.tile([P, N], F32)
         nc.vector.tensor_copy(out=bias_all[:], in_=acc[0][:])
 
-        for n in range(ROUNDS):
+        for n in range(PASSES):
             step(n)
 
         for m in range(M_TILES):

from contextlib import ExitStack

import concourse.mybir as mybir
from concourse.masks import make_identity

F32 = mybir.dt.float32
BF16 = mybir.dt.bfloat16
U32 = mybir.dt.uint32
U8 = mybir.dt.uint8
FP8X4 = mybir.dt.float8_e4m3fn_x4

P = 128
PACK = 4
HALVES = 2
K_PASS = P * PACK
ROWS = 512
K = 16384
N = 512
M_TILES = ROWS // P
PASSES = K // K_PASS
CHUNK_PASSES = 4
CHUNK_K = CHUNK_PASSES * K_PASS
UNITS = M_TILES * (PASSES // CHUNK_PASSES)
BANK_PASSES = 2
UNIT_BANKS = CHUNK_PASSES // BANK_PASSES

QUANTISE_AHEAD = M_TILES - 1
COPY_AHEAD = QUANTISE_AHEAD + 1
TRANSPOSE_AHEAD = COPY_AHEAD + 1
X_BUFS = 8
GROUPS_AHEAD = X_BUFS + TRANSPOSE_AHEAD - QUANTISE_AHEAD
W_BUFS = GROUPS_AHEAD
SCALAR_COLS = 192

FLOPS = 2 * ROWS * K * N


def tile_bitlinear_k_kernel(tc, x, kernel, bias, out):
    nc = tc.nc
    x_rows = x.flatten_outer_dims()
    out_rows = out.flatten_outer_dims()

    with ExitStack() as ctx:
        const = ctx.enter_context(tc.tile_pool(name="const", bufs=1))
        x_loaded = ctx.enter_context(tc.tile_pool(name="x_loaded", bufs=X_BUFS))
        w_loaded = ctx.enter_context(tc.tile_pool(name="w_loaded", bufs=W_BUFS))
        grouped = ctx.enter_context(tc.tile_pool(name="grouped", bufs=3))
        w_quant = ctx.enter_context(tc.tile_pool(name="w_quant", bufs=3))
        x_quant = ctx.enter_context(tc.tile_pool(name="x_quant", bufs=2 * M_TILES))
        results = ctx.enter_context(tc.tile_pool(name="results", bufs=M_TILES))
        psum_t = ctx.enter_context(tc.psum_pool(name="psum_t", bufs=2 * UNIT_BANKS))
        psum_acc = ctx.enter_context(tc.psum_pool(name="psum_acc", bufs=1))
        ctx.enter_context(tc.manual_schedule())

        x_raw_of = {}
        w_raw_of = {}
        banks_of = {}
        x_grouped_of = {}
        w_grouped_of = {}
        x_codes_of = {}
        x_scales_of = {}
        w_codes_of = {}
        w_scales_of = {}

        def load_x(unit):
            chunk, m = divmod(unit, M_TILES)
            x_raw = x_loaded.tile([P, CHUNK_K], BF16)
            nc.sync.dma_start(
                out=x_raw[:],
                in_=x_rows[m * P : (m + 1) * P, chunk * CHUNK_K : (chunk + 1) * CHUNK_K],
            )
            x_raw_of[unit] = x_raw

        def load_w(g):
            w_raw = w_loaded.tile([P, PACK, N], BF16)
            nc.sync.dma_start(
                out=w_raw[:].rearrange("p (h e) n -> p h e n", h=HALVES),
                in_=kernel[g * K_PASS : (g + 1) * K_PASS, :].rearrange(
                    "(h p e) n -> p h e n", h=HALVES, p=P
                ),
            )
            w_raw_of[g] = w_raw

        def load_group(g):
            if 0 <= g + QUANTISE_AHEAD < UNITS:
                load_x(g + QUANTISE_AHEAD)
            if 0 <= g < PASSES:
                load_w(g)

        def transpose_x(unit):
            words = x_raw_of[unit][:].bitcast(F32)
            banks = []
            for b in range(UNIT_BANKS):
                bank = psum_t.tile([P, BANK_PASSES, HALVES, P], F32)
                for a in range(BANK_PASSES):
                    for h in range(HALVES):
                        j = (b * BANK_PASSES + a) * HALVES + h
                        nc.tensor.transpose(
                            bank[:, a, h, :], words[:, j * P : (j + 1) * P], ident[:]
                        )
                banks.append(bank)
            banks_of[unit] = banks

        def copy_x(unit):
            x_grouped = grouped.tile([P, CHUNK_PASSES, P, PACK], BF16, align_bytes=64)
            for b in range(UNIT_BANKS):
                nc.scalar.copy(
                    out=x_grouped[:, b * BANK_PASSES : (b + 1) * BANK_PASSES].bitcast(F32),
                    in_=banks_of[unit][b][:].rearrange("p a h r -> p a r h"),
                )
            x_grouped_of[unit] = x_grouped

        def quantise_x(unit):
            x_codes = x_quant.tile([P, CHUNK_PASSES, P], U32, align_bytes=64)
            x_scales = x_quant.tile([P, CHUNK_PASSES, P], U8, align_bytes=64)
            nc.vector.quantize_mx(
                out=x_codes[:].rearrange("p a r -> p (a r)").bitcast(FP8X4),
                scales=x_scales[:].rearrange("p a r -> p (a r)"),
                in_=x_grouped_of[unit][:].rearrange("p a r t -> p (a r t)"),
            )
            x_codes_of[unit] = x_codes
            x_scales_of[unit] = x_scales

        def regroup_w(g):
            w_raw = w_raw_of[g]
            w_grouped = grouped.tile([P, N, PACK], BF16, align_bytes=64)
            nc.scalar.copy(
                out=w_grouped[:, :SCALAR_COLS, :].rearrange("p (c j) t -> p c t j", j=4),
                in_=w_raw[:, :, :SCALAR_COLS].rearrange("p t (c j) -> p c t j", j=4),
            )
            nc.vector.tensor_copy(
                out=w_grouped[:, SCALAR_COLS:, :].rearrange("p (c j) t -> p c t j", j=4),
                in_=w_raw[:, :, SCALAR_COLS:].rearrange("p t (c j) -> p c t j", j=4),
            )
            w_grouped_of[g] = w_grouped

        def quantise_w(g):
            w_codes = w_quant.tile([P, N], U32, align_bytes=64)
            w_scales = w_quant.tile([P, N], U8, align_bytes=64)
            nc.vector.quantize_mx(
                out=w_codes[:].bitcast(FP8X4),
                scales=w_scales[:],
                in_=w_grouped_of[g][:].rearrange("p n t -> p (n t)"),
            )
            w_codes_of[g] = w_codes
            w_scales_of[g] = w_scales

        def multiply(g):
            chunk, a = divmod(g, CHUNK_PASSES)
            for m in range(M_TILES):
                unit = chunk * M_TILES + m
                nc.tensor.matmul_mx(
                    out=acc[m][:],
                    lhsT=x_codes_of[unit][:, a, :].bitcast(FP8X4),
                    lhsT_scale=x_scales_of[unit][:, a, :],
                    rhs=w_codes_of[g][:].bitcast(FP8X4),
                    rhs_scale=w_scales_of[g][:],
                    start=(g == 0),
                    stop=(g == PASSES - 1),
                )

        def step(n):
            if n + TRANSPOSE_AHEAD < UNITS:
                transpose_x(n + TRANSPOSE_AHEAD)
            if n >= 0:
                regroup_w(n)
            if 0 <= n + COPY_AHEAD < UNITS:
                copy_x(n + COPY_AHEAD)
            if 0 <= n + QUANTISE_AHEAD < UNITS:
                quantise_x(n + QUANTISE_AHEAD)
            if n >= 0:
                quantise_w(n)
                multiply(n)
            load_group(n + GROUPS_AHEAD)

        first_step = -TRANSPOSE_AHEAD
        for g in range(first_step, first_step + GROUPS_AHEAD):
            load_group(g)

        ident = const.tile([P, P], F32)
        make_identity(nc, ident[:])
        ones = const.tile([P, P], BF16)
        nc.vector.memset(ones[:], 1.0)
        bias_row = const.tile([P, N], BF16)
        nc.vector.memset(bias_row[:], 0.0)
        nc.scalar.dma_start(out=bias_row[0:1, :], in_=bias.rearrange("(o n) -> o n", o=1))

        acc = []
        for m in range(M_TILES):
            acc_m = psum_acc.tile([P, N], F32, name="acc%d" % m)
            acc.append(acc_m)

        for n in range(first_step, 0):
            step(n)

        nc.tensor.matmul(out=acc[0][:], lhsT=ones[:], rhs=bias_row[:], start=True, stop=True)
        bias_all = const.tile([P, N], F32)
        nc.vector.tensor_copy(out=bias_all[:], in_=acc[0][:])

        for n in range(PASSES):
            step(n)

        for m in range(M_TILES):
            result = results.tile([P, N], F32)
            nc.vector.tensor_tensor(
                out=result[:], in0=acc[m][:], in1=bias_all[:], op=mybir.AluOpType.add
            )
            nc.sync.dma_start(out=out_rows[m * P : (m + 1) * P, :], in_=result[:])
